import numpy as np
import ml_dtypes


def mxq(x, axis, fmt="e4m3"):
    dtype, down = {"e4m3": (ml_dtypes.float8_e4m3fn, 7), "e5m2": (ml_dtypes.float8_e5m2, 14)}[fmt]
    v = np.moveaxis(np.asarray(x, np.float32).astype(ml_dtypes.bfloat16).astype(np.float64), axis, -1)
    blocks = v.reshape(v.shape[:-1] + (-1, 32))
    amax = np.abs(blocks).max(-1, keepdims=True)
    byte = np.maximum(np.where(amax > 0, np.frexp(amax)[1] - 1 + 127, 0) - down, 1)
    scale = np.exp2(byte - 127.0)
    codes = (blocks / scale).astype(np.float32).astype(dtype).astype(np.float64)
    return np.moveaxis((codes * scale).reshape(v.shape), -1, axis)


WIDE = False


def mx_kscale(k):
    if not WIDE:
        return np.ones(k)
    levels = np.array([10, -10, 5, -5, 0])
    a = np.random.permutation(np.resize(levels, k // 512 * 4)).reshape(k // 512, 4)
    idx = np.arange(k)
    return np.exp2(a[idx // 512, idx % 128 // 32])


BF16 = ml_dtypes.bfloat16


def bf(x):
    return np.asarray(x, np.float32).astype(BF16)


def f64(x):
    return np.asarray(x).astype(np.float64)


B, N, F = 16, 512, 512


def setup_inputs():
    s = mx_kscale(N)
    return {"regional_means": bf(np.random.standard_normal((B, N, F)) * (4.0 / np.sqrt(N)) / s[:, None]),
            "adj": bf(np.random.uniform(0.0, 1.0, (B, N, N)) * s)}


def reference(regional_means, adj):
    n = adj.shape[-1]
    mask = 1.0 - np.eye(n)
    adj_masked = f64(adj) * mask
    return mxq(adj_masked, 2, "e4m3") @ mxq(f64(regional_means), 1, "e4m3")

@@ -1,0 +1,143 @@
+from contextlib import ExitStack
+
+import concourse.mybir as mybir
+from concourse.masks import make_identity
+
+BF16 = mybir.dt.bfloat16
+F32 = mybir.dt.float32
+U32 = mybir.dt.uint32
+U8 = mybir.dt.uint8
+FP8X4 = mybir.dt.float8_e4m3fn_x4
+MULT = mybir.AluOpType.mult
+ADD = mybir.AluOpType.add
+
+P = 128
+PACK = 4
+B, N, F = 16, 512, 512
+FLOPS = 2 * B * N * N * F
+
+LEAD = 12
+OUT_BUFS = 8
+
+
+def tile_gcn_t_kernel(tc, regional_means, adj, out):
+    nc = tc.nc
+    with ExitStack() as ctx:
+        const = ctx.enter_context(tc.tile_pool(name="const", bufs=1))
+        a_pool = ctx.enter_context(tc.tile_pool(name="a_in", bufs=LEAD))
+        r_pool = ctx.enter_context(tc.tile_pool(name="r_in", bufs=LEAD))
+        g_pool = ctx.enter_context(tc.tile_pool(name="grouped", bufs=3))
+        q_pool = ctx.enter_context(tc.tile_pool(name="quant", bufs=3))
+        o_pool = ctx.enter_context(tc.tile_pool(name="o_out", bufs=OUT_BUFS))
+        ps_t = ctx.enter_context(tc.psum_pool(name="ps_t", bufs=4))
+        ps_o = ctx.enter_context(tc.psum_pool(name="ps_o", bufs=4))
+        ctx.enter_context(tc.manual_schedule())
+
+        a_in = {}
+        r_in = {}
+        banks_t = {}
+        g_a = {}
+        g_r = {}
+        q_a = {}
+        q_r = {}
+
+        def load(b):
+            a = a_pool.tile([P, PACK * N], BF16, name="a")
+            nc.sync.dma_start(out=a[:], in_=adj[b].rearrange("(p t) j -> p (t j)", t=PACK))
+            a_in[b] = a
+            r = r_pool.tile([P, PACK * F], BF16, name="r")
+            nc.sync.dma_start(
+                out=r[:], in_=regional_means[b].rearrange("(p t) f -> p (t f)", t=PACK)
+            )
+            r_in[b] = r
+
+        for b in range(LEAD):
+            load(b)
+
+        ident = const.tile([P, P], F32, name="ident")
+        make_identity(nc, ident[:])
+        mask = const.tile([P, PACK, P, PACK], BF16, name="mask")
+        nc.vector.memset(mask[:], 1.0)
+        for t in range(PACK):
+            nc.vector.tensor_scalar(
+                out=mask[:, t, :, t], in0=ident[:], scalar1=-1.0, scalar2=1.0, op0=MULT, op1=ADD
+            )
+        mask_flat = mask[:].rearrange("p t c s -> p (t c s)")
+
+        def mask_mul(b):
+            a = a_in[b]
+            nc.vector.tensor_tensor(out=a[:], in0=a[:], in1=mask_flat, op=MULT)
+
+        def transposes(b):
+            words = a_in[b][:].bitcast(F32).rearrange("p (t c u) -> p t c u", t=PACK, u=2)
+            banks = []
+            for h in range(2):
+                bank = ps_t.tile([P, 2, 2, P], F32, name="bank_t")
+                for t2 in range(2):
+                    for u in range(2):
+                        nc.tensor.transpose(bank[:, t2, u, :], words[:, 2 * h + t2, :, u], ident[:])
+                banks.append(bank)
+            banks_t[b] = banks
+
+        def copy_t(b):
+            ga = g_pool.tile([P, PACK * P * PACK], BF16, name="ga", align_bytes=64)
+            ga_words = ga[:].bitcast(F32).rearrange("q (t m u) -> q t m u", t=PACK, u=2)
+            for h in range(2):
+                nc.scalar.copy(
+                    out=ga_words[:, 2 * h : 2 * h + 2, :, :],
+                    in_=banks_t[b][h][:].rearrange("q t u m -> q t m u"),
+                )
+            g_a[b] = ga
+
+        def regroup(b):
+            gr = g_pool.tile([P, F * PACK], BF16, name="gr", align_bytes=64)
+            nc.vector.tensor_copy(
+                out=gr[:].rearrange("p (c i t) -> p c t i", i=4, t=PACK),
+                in_=r_in[b][:].rearrange("p (t c i) -> p c t i", t=PACK, i=4),
+            )
+            g_r[b] = gr
+
+        def quantise(grouped, width, label):
+            codes = q_pool.tile([P, width], U32, name="codes_" + label, align_bytes=64)
+            scales = q_pool.tile([P, width], U8, name="scales_" + label, align_bytes=64)
+            nc.vector.quantize_mx(out=codes[:].bitcast(FP8X4), scales=scales[:], in_=grouped[:])
+            return codes, scales
+
+        def multiply_and_store(b):
+            ca, sa = q_a[b]
+            cr, sr = q_r[b]
+            o = o_pool.tile([P, PACK * F], F32, name="o")
+            accs = []
+            for t in range(PACK):
+                acc = ps_o.tile([P, F], F32, name="acc")
+                cols = slice(t * P, (t + 1) * P)
+                nc.tensor.matmul_mx(
+                    out=acc[:],
+                    lhsT=ca[:, cols].bitcast(FP8X4),
+                    lhsT_scale=sa[:, cols],
+                    rhs=cr[:].bitcast(FP8X4),
+                    rhs_scale=sr[:],
+                    start=True,
+                    stop=True,
+                )
+                accs.append(acc)
+            for t in range(PACK):
+                nc.scalar.copy(out=o[:, t * F : (t + 1) * F], in_=accs[t][:])
+            nc.sync.dma_start(out=out[b].rearrange("(p t) f -> p (t f)", t=PACK), in_=o[:])
+
+        mask_mul(0)
+        transposes(0)
+        copy_t(0)
+        regroup(0)
+        for b in range(B):
+            if b + 1 < B:
+                mask_mul(b + 1)
+                transposes(b + 1)
+            q_a[b] = quantise(g_a[b], N, "a")
+            q_r[b] = quantise(g_r[b], F, "r")
+            if b + 1 < B:
+                copy_t(b + 1)
+                regroup(b + 1)
+            multiply_and_store(b)
+            if b + LEAD < B:
+                load(b + LEAD)

@@ -123,7 +123,7 @@ def tile_gcn_t_kernel(tc, regional_means, adj, out):
                 accs.append(acc)
             for t in range(PACK):
                 nc.scalar.copy(out=o[:, t * F : (t + 1) * F], in_=accs[t][:])
-            nc.sync.dma_start(out=out[b].rearrange("(p t) f -> p (t f)", t=PACK), in_=o[:])
+            nc.gpsimd.dma_start(out=out[b].rearrange("(p t) f -> p (t f)", t=PACK), in_=o[:])
 
         mask_mul(0)
         transposes(0)

@@ -16,100 +16,130 @@ PACK = 4
 B, N, F = 16, 512, 512
 FLOPS = 2 * B * N * N * F
 
-LEAD = 12
-OUT_BUFS = 8
+H = P // B
+CHUNKS = 4
+ROWS = N // H // CHUNKS
+MM = N // H // PACK
+R_BUFS = 8
 
 
 def tile_gcn_t_kernel(tc, regional_means, adj, out):
     nc = tc.nc
     with ExitStack() as ctx:
         const = ctx.enter_context(tc.tile_pool(name="const", bufs=1))
-        a_pool = ctx.enter_context(tc.tile_pool(name="a_in", bufs=LEAD))
-        r_pool = ctx.enter_context(tc.tile_pool(name="r_in", bufs=LEAD))
-        g_pool = ctx.enter_context(tc.tile_pool(name="grouped", bufs=3))
-        q_pool = ctx.enter_context(tc.tile_pool(name="quant", bufs=3))
-        o_pool = ctx.enter_context(tc.tile_pool(name="o_out", bufs=OUT_BUFS))
-        ps_t = ctx.enter_context(tc.psum_pool(name="ps_t", bufs=4))
-        ps_o = ctx.enter_context(tc.psum_pool(name="ps_o", bufs=4))
+        big = ctx.enter_context(tc.tile_pool(name="big", bufs=CHUNKS))
+        ga_pool = ctx.enter_context(tc.tile_pool(name="ga", bufs=1))
+        r_pool = ctx.enter_context(tc.tile_pool(name="r_in", bufs=R_BUFS))
+        gr_pool = ctx.enter_context(tc.tile_pool(name="gr", bufs=3))
+        qa_pool = ctx.enter_context(tc.tile_pool(name="qa", bufs=3))
+        qr_pool = ctx.enter_context(tc.tile_pool(name="qr", bufs=4))
+        psum = ctx.enter_context(tc.psum_pool(name="psum", bufs=8))
         ctx.enter_context(tc.manual_schedule())
 
-        a_in = {}
+        adj_rows = adj.rearrange("b (h r) j -> (b h) (r j)", h=H)
+        chunk_cols = ROWS * N
+        chunks = []
+        for c in range(CHUNKS):
+            ch = big.tile([P, ROWS * (N + 1) + 3 * ROWS], BF16, name="chunk", tag="big")
+            nc.sync.dma_start(
+                out=ch[:, 0:chunk_cols], in_=adj_rows[:, c * chunk_cols : (c + 1) * chunk_cols]
+            )
+            chunks.append(ch)
+
         r_in = {}
-        banks_t = {}
-        g_a = {}
         g_r = {}
-        q_a = {}
         q_r = {}
 
-        def load(b):
-            a = a_pool.tile([P, PACK * N], BF16, name="a")
-            nc.sync.dma_start(out=a[:], in_=adj[b].rearrange("(p t) j -> p (t j)", t=PACK))
-            a_in[b] = a
+        def load_r(b):
             r = r_pool.tile([P, PACK * F], BF16, name="r")
             nc.sync.dma_start(
                 out=r[:], in_=regional_means[b].rearrange("(p t) f -> p (t f)", t=PACK)
             )
             r_in[b] = r
 
-        for b in range(LEAD):
-            load(b)
+        for b in range(R_BUFS):
+            load_r(b)
 
         ident = const.tile([P, P], F32, name="ident")
         make_identity(nc, ident[:])
-        mask = const.tile([P, PACK, P, PACK], BF16, name="mask")
-        nc.vector.memset(mask[:], 1.0)
-        for t in range(PACK):
-            nc.vector.tensor_scalar(
-                out=mask[:, t, :, t], in0=ident[:], scalar1=-1.0, scalar2=1.0, op0=MULT, op1=ADD
+        hit = const.tile([P, H], F32, name="hit")
+        nc.vector.tensor_reduce(
+            out=hit[:],
+            in_=ident[:].rearrange("p (b c) -> p c b", c=H),
+            axis=mybir.AxisListType.X,
+            op=ADD,
+        )
+        keep = const.tile([P, H], BF16, name="keep")
+        nc.vector.tensor_scalar(
+            out=keep[:], in0=hit[:], scalar1=-1.0, scalar2=1.0, op0=MULT, op1=ADD
+        )
+        keep_rows = keep[:].unsqueeze(1).to_broadcast([P, ROWS, H])
+
+        ga_all = ga_pool.tile([P, B * PACK * P * PACK], BF16, name="ga_all", align_bytes=64)
+        ga_words = ga_all[:].bitcast(F32).rearrange(
+            "q (b t h m u) -> q b t h m u", b=B, t=PACK, h=H, u=2
+        )
+
+        for c in range(CHUNKS):
+            ch = chunks[c]
+            start = ROWS * c
+            diag = (
+                ch[:, start : start + ROWS * (N + 1)]
+                .rearrange("p (r x) -> p r x", x=N + 1)[:, :, 0:N]
+                .rearrange("p r (x y) -> p r x y", x=H)[:, :, :, 0]
             )
-        mask_flat = mask[:].rearrange("p t c s -> p (t c s)")
-
-        def mask_mul(b):
-            a = a_in[b]
-            nc.vector.tensor_tensor(out=a[:], in0=a[:], in1=mask_flat, op=MULT)
-
-        def transposes(b):
-            words = a_in[b][:].bitcast(F32).rearrange("p (t c u) -> p t c u", t=PACK, u=2)
-            banks = []
-            for h in range(2):
-                bank = ps_t.tile([P, 2, 2, P], F32, name="bank_t")
-                for t2 in range(2):
-                    for u in range(2):
-                        nc.tensor.transpose(bank[:, t2, u, :], words[:, 2 * h + t2, :, u], ident[:])
-                banks.append(bank)
-            banks_t[b] = banks
-
-        def copy_t(b):
-            ga = g_pool.tile([P, PACK * P * PACK], BF16, name="ga", align_bytes=64)
-            ga_words = ga[:].bitcast(F32).rearrange("q (t m u) -> q t m u", t=PACK, u=2)
-            for h in range(2):
-                nc.scalar.copy(
-                    out=ga_words[:, 2 * h : 2 * h + 2, :, :],
-                    in_=banks_t[b][h][:].rearrange("q t u m -> q t m u"),
-                )
-            g_a[b] = ga
+            nc.vector.tensor_tensor(out=diag, in0=diag, in1=keep_rows, op=MULT)
+            words = ch[:, 0:chunk_cols].bitcast(F32).rearrange("p (r c u) -> p r c u", r=ROWS, u=2)
+            for t in range(PACK):
+                for mp in range(2):
+                    bank = psum.tile([P, 2, 2, P], F32, name="bank", tag="bank")
+                    for m2 in range(2):
+                        for u in range(2):
+                            nc.tensor.transpose(
+                                bank[:, m2, u, :],
+                                words[:, PACK * (2 * mp + m2) + t, :, u],
+                                ident[:],
+                            )
+                    m0 = PACK * c + 2 * mp
+                    nc.scalar.copy(
+                        out=ga_words[:, :, t, :, m0 : m0 + 2, :],
+                        in_=bank[:].rearrange("q m u (b h) -> q b h m u", h=H),
+                    )
 
         def regroup(b):
-            gr = g_pool.tile([P, F * PACK], BF16, name="gr", align_bytes=64)
+            gr = gr_pool.tile([P, F * PACK], BF16, name="gr", align_bytes=64)
             nc.vector.tensor_copy(
                 out=gr[:].rearrange("p (c i t) -> p c t i", i=4, t=PACK),
                 in_=r_in[b][:].rearrange("p (t c i) -> p c t i", t=PACK, i=4),
             )
             g_r[b] = gr
 
-        def quantise(grouped, width, label):
-            codes = q_pool.tile([P, width], U32, name="codes_" + label, align_bytes=64)
-            scales = q_pool.tile([P, width], U8, name="scales_" + label, align_bytes=64)
-            nc.vector.quantize_mx(out=codes[:].bitcast(FP8X4), scales=scales[:], in_=grouped[:])
+        def quantise(pool, grouped, width, label):
+            codes = pool.tile([P, width], U32, name="codes_" + label, align_bytes=64)
+            scales = pool.tile([P, width], U8, name="scales_" + label, align_bytes=64)
+            nc.vector.quantize_mx(out=codes[:].bitcast(FP8X4), scales=scales[:], in_=grouped)
             return codes, scales
 
-        def multiply_and_store(b):
-            ca, sa = q_a[b]
+        regroup(0)
+        regroup(1)
+        q_r[0] = quantise(qr_pool, g_r[0][:], F, "r")
+        regroup(2)
+        q_r[1] = quantise(qr_pool, g_r[1][:], F, "r")
+
+        o_pair = None
+        for b in range(B):
+            width = PACK * P * PACK
+            ca, sa = quantise(qa_pool, ga_all[:, b * width : (b + 1) * width], N, "a")
+            if b + 3 < B:
+                regroup(b + 3)
+            if b + 2 < B:
+                q_r[b + 2] = quantise(qr_pool, g_r[b + 2][:], F, "r")
             cr, sr = q_r[b]
-            o = o_pool.tile([P, PACK * F], F32, name="o")
+            if b % 2 == 0:
+                o_pair = big.tile([P, 2, PACK * F], F32, name="o_pair", tag="big")
             accs = []
             for t in range(PACK):
-                acc = ps_o.tile([P, F], F32, name="acc")
+                acc = psum.tile([P, F], F32, name="acc", tag="bank")
                 cols = slice(t * P, (t + 1) * P)
                 nc.tensor.matmul_mx(
                     out=acc[:],
@@ -122,22 +152,9 @@ def tile_gcn_t_kernel(tc, regional_means, adj, out):
                 )
                 accs.append(acc)
             for t in range(PACK):
-                nc.scalar.copy(out=o[:, t * F : (t + 1) * F], in_=accs[t][:])
-            nc.gpsimd.dma_start(out=out[b].rearrange("(p t) f -> p (t f)", t=PACK), in_=o[:])
-
-        mask_mul(0)
-        transposes(0)
-        copy_t(0)
-        regroup(0)
-        for b in range(B):
-            if b + 1 < B:
-                mask_mul(b + 1)
-                transposes(b + 1)
-            q_a[b] = quantise(g_a[b], N, "a")
-            q_r[b] = quantise(g_r[b], F, "r")
-            if b + 1 < B:
-                copy_t(b + 1)
-                regroup(b + 1)
-            multiply_and_store(b)
-            if b + LEAD < B:
-                load(b + LEAD)
+                nc.scalar.copy(out=o_pair[:, b % 2, t * F : (t + 1) * F], in_=accs[t][:])
+            nc.sync.dma_start(
+                out=out[b].rearrange("(p t) f -> p (t f)", t=PACK), in_=o_pair[:, b % 2, :]
+            )
+            if b + R_BUFS < B:
+                load_r(b + R_BUFS)

@@ -16,39 +16,40 @@ PACK = 4
 B, N, F = 16, 512, 512
 FLOPS = 2 * B * N * N * F
 
-H = P // B
-CHUNKS = 4
-ROWS = N // H // CHUNKS
-MM = N // H // PACK
-R_BUFS = 8
+G = 4
+GROUPS = B // G
+S = P // G
+ROWS = N // S
+R_BUFS = 12
+OUT_BUFS = 8
 
 
 def tile_gcn_t_kernel(tc, regional_means, adj, out):
     nc = tc.nc
     with ExitStack() as ctx:
         const = ctx.enter_context(tc.tile_pool(name="const", bufs=1))
-        big = ctx.enter_context(tc.tile_pool(name="big", bufs=CHUNKS))
-        ga_pool = ctx.enter_context(tc.tile_pool(name="ga", bufs=1))
+        a_pool = ctx.enter_context(tc.tile_pool(name="a_in", bufs=3))
         r_pool = ctx.enter_context(tc.tile_pool(name="r_in", bufs=R_BUFS))
+        ga_pool = ctx.enter_context(tc.tile_pool(name="ga", bufs=2))
         gr_pool = ctx.enter_context(tc.tile_pool(name="gr", bufs=3))
-        qa_pool = ctx.enter_context(tc.tile_pool(name="qa", bufs=3))
-        qr_pool = ctx.enter_context(tc.tile_pool(name="qr", bufs=4))
-        psum = ctx.enter_context(tc.psum_pool(name="psum", bufs=8))
+        q_pool = ctx.enter_context(tc.tile_pool(name="quant", bufs=3))
+        o_pool = ctx.enter_context(tc.tile_pool(name="o_out", bufs=OUT_BUFS))
+        ps_t = ctx.enter_context(tc.psum_pool(name="ps_t", bufs=4))
+        ps_o = ctx.enter_context(tc.psum_pool(name="ps_o", bufs=4))
         ctx.enter_context(tc.manual_schedule())
 
-        adj_rows = adj.rearrange("b (h r) j -> (b h) (r j)", h=H)
-        chunk_cols = ROWS * N
-        chunks = []
-        for c in range(CHUNKS):
-            ch = big.tile([P, ROWS * (N + 1) + 3 * ROWS], BF16, name="chunk", tag="big")
-            nc.sync.dma_start(
-                out=ch[:, 0:chunk_cols], in_=adj_rows[:, c * chunk_cols : (c + 1) * chunk_cols]
-            )
-            chunks.append(ch)
-
+        a_in = {}
         r_in = {}
+        g_a = {}
         g_r = {}
-        q_r = {}
+
+        def load_group(g):
+            ag = a_pool.tile([P, ROWS * (N + 1)], BF16, name="ag")
+            nc.sync.dma_start(
+                out=ag[:, 0 : ROWS * N],
+                in_=adj[G * g : G * g + G].rearrange("b (s r) j -> (b s) (r j)", s=S),
+            )
+            a_in[g] = ag
 
         def load_r(b):
             r = r_pool.tile([P, PACK * F], BF16, name="r")
@@ -57,54 +58,59 @@ def tile_gcn_t_kernel(tc, regional_means, adj, out):
             )
             r_in[b] = r
 
-        for b in range(R_BUFS):
+        load_group(0)
+        load_r(0)
+        load_group(1)
+        for b in range(1, 6):
             load_r(b)
+        load_group(2)
+        for b in range(6, R_BUFS):
+            load_r(b)
+        late_loads = [(load_group, 3), (load_r, 12), (load_r, 13), (load_r, 14), (load_r, 15)]
 
         ident = const.tile([P, P], F32, name="ident")
         make_identity(nc, ident[:])
-        hit = const.tile([P, H], F32, name="hit")
+        hit = const.tile([P, S], F32, name="hit")
         nc.vector.tensor_reduce(
             out=hit[:],
-            in_=ident[:].rearrange("p (b c) -> p c b", c=H),
+            in_=ident[:].rearrange("p (b c) -> p c b", c=S),
             axis=mybir.AxisListType.X,
             op=ADD,
         )
-        keep = const.tile([P, H], BF16, name="keep")
+        keep = const.tile([P, S], BF16, name="keep")
         nc.vector.tensor_scalar(
             out=keep[:], in0=hit[:], scalar1=-1.0, scalar2=1.0, op0=MULT, op1=ADD
         )
-        keep_rows = keep[:].unsqueeze(1).to_broadcast([P, ROWS, H])
+        keep_rows = keep[:].unsqueeze(1).to_broadcast([P, PACK, S])
 
-        ga_all = ga_pool.tile([P, B * PACK * P * PACK], BF16, name="ga_all", align_bytes=64)
-        ga_words = ga_all[:].bitcast(F32).rearrange(
-            "q (b t h m u) -> q b t h m u", b=B, t=PACK, h=H, u=2
-        )
-
-        for c in range(CHUNKS):
-            ch = chunks[c]
-            start = ROWS * c
+        def part(g, t):
+            ag = a_in[g]
+            if t == 0:
+                g_a[g] = ga_pool.tile([P, G * PACK * P * PACK], BF16, name="ga", align_bytes=64)
+            ga_words = g_a[g][:].bitcast(F32).rearrange(
+                "q (b t s m u) -> q b t s m u", b=G, t=PACK, s=S, u=2
+            )
             diag = (
-                ch[:, start : start + ROWS * (N + 1)]
+                ag[:]
                 .rearrange("p (r x) -> p r x", x=N + 1)[:, :, 0:N]
-                .rearrange("p r (x y) -> p r x y", x=H)[:, :, :, 0]
+                .rearrange("p r (c y) -> p r c y", c=S)[:, :, :, 0]
+                .rearrange("p (m t) c -> p m t c", t=PACK)[:, :, t, :]
             )
             nc.vector.tensor_tensor(out=diag, in0=diag, in1=keep_rows, op=MULT)
-            words = ch[:, 0:chunk_cols].bitcast(F32).rearrange("p (r c u) -> p r c u", r=ROWS, u=2)
-            for t in range(PACK):
-                for mp in range(2):
-                    bank = psum.tile([P, 2, 2, P], F32, name="bank", tag="bank")
-                    for m2 in range(2):
-                        for u in range(2):
-                            nc.tensor.transpose(
-                                bank[:, m2, u, :],
-                                words[:, PACK * (2 * mp + m2) + t, :, u],
-                                ident[:],
-                            )
-                    m0 = PACK * c + 2 * mp
-                    nc.scalar.copy(
-                        out=ga_words[:, :, t, :, m0 : m0 + 2, :],
-                        in_=bank[:].rearrange("q m u (b h) -> q b h m u", h=H),
-                    )
+            words = ag[:, 0 : ROWS * N].bitcast(F32).rearrange("p (r c u) -> p r c u", r=ROWS, u=2)
+            for mh in range(2):
+                bank = ps_t.tile([P, 2, 2, P], F32, name="bank_t")
+                for m2 in range(2):
+                    for u in range(2):
+                        nc.tensor.transpose(
+                            bank[:, m2, u, :], words[:, PACK * (2 * mh + m2) + t, :, u], ident[:]
+                        )
+                dst = ga_words[:, :, t, :, 2 * mh : 2 * mh + 2, :]
+                src = bank[:].rearrange("q m u (b s) -> q b s m u", s=S)
+                if t == PACK - 1:
+                    nc.vector.tensor_copy(out=dst, in_=src)
+                else:
+                    nc.scalar.copy(out=dst, in_=src)
 
         def regroup(b):
             gr = gr_pool.tile([P, F * PACK], BF16, name="gr", align_bytes=64)
@@ -114,32 +120,17 @@ def tile_gcn_t_kernel(tc, regional_means, adj, out):
             )
             g_r[b] = gr
 
-        def quantise(pool, grouped, width, label):
-            codes = pool.tile([P, width], U32, name="codes_" + label, align_bytes=64)
-            scales = pool.tile([P, width], U8, name="scales_" + label, align_bytes=64)
+        def quantise(grouped, width, label):
+            codes = q_pool.tile([P, width], U32, name="codes_" + label, align_bytes=64)
+            scales = q_pool.tile([P, width], U8, name="scales_" + label, align_bytes=64)
             nc.vector.quantize_mx(out=codes[:].bitcast(FP8X4), scales=scales[:], in_=grouped)
             return codes, scales
 
-        regroup(0)
-        regroup(1)
-        q_r[0] = quantise(qr_pool, g_r[0][:], F, "r")
-        regroup(2)
-        q_r[1] = quantise(qr_pool, g_r[1][:], F, "r")
-
-        o_pair = None
-        for b in range(B):
-            width = PACK * P * PACK
-            ca, sa = quantise(qa_pool, ga_all[:, b * width : (b + 1) * width], N, "a")
-            if b + 3 < B:
-                regroup(b + 3)
-            if b + 2 < B:
-                q_r[b + 2] = quantise(qr_pool, g_r[b + 2][:], F, "r")
-            cr, sr = q_r[b]
-            if b % 2 == 0:
-                o_pair = big.tile([P, 2, PACK * F], F32, name="o_pair", tag="big")
+        def multiply_and_store(b, ca, sa, cr, sr):
+            o = o_pool.tile([P, PACK * F], F32, name="o")
             accs = []
             for t in range(PACK):
-                acc = psum.tile([P, F], F32, name="acc", tag="bank")
+                acc = ps_o.tile([P, F], F32, name="acc")
                 cols = slice(t * P, (t + 1) * P)
                 nc.tensor.matmul_mx(
                     out=acc[:],
@@ -152,9 +143,22 @@ def tile_gcn_t_kernel(tc, regional_means, adj, out):
                 )
                 accs.append(acc)
             for t in range(PACK):
-                nc.scalar.copy(out=o_pair[:, b % 2, t * F : (t + 1) * F], in_=accs[t][:])
-            nc.sync.dma_start(
-                out=out[b].rearrange("(p t) f -> p (t f)", t=PACK), in_=o_pair[:, b % 2, :]
-            )
-            if b + R_BUFS < B:
-                load_r(b + R_BUFS)
+                nc.scalar.copy(out=o[:, t * F : (t + 1) * F], in_=accs[t][:])
+            nc.sync.dma_start(out=out[b].rearrange("(p t) f -> p (t f)", t=PACK), in_=o[:])
+
+        for t in range(PACK):
+            part(0, t)
+        regroup(0)
+        width = PACK * P * PACK
+        for b in range(B):
+            g, k = divmod(b, G)
+            if g + 1 < GROUPS:
+                part(g + 1, k)
+            ca, sa = quantise(g_a[g][:, k * width : (k + 1) * width], N, "a")
+            cr, sr = quantise(g_r[b][:], F, "r")
+            if b + 1 < B:
+                regroup(b + 1)
+            multiply_and_store(b, ca, sa, cr, sr)
+            if b < len(late_loads):
+                fn, arg = late_loads[b]
+                fn(arg)

@@ -16,11 +16,7 @@ PACK = 4
 B, N, F = 16, 512, 512
 FLOPS = 2 * B * N * N * F
 
-G = 4
-GROUPS = B // G
-S = P // G
-ROWS = N // S
-R_BUFS = 12
+LEAD = 12
 OUT_BUFS = 8
 
 
@@ -28,92 +24,72 @@ def tile_gcn_t_kernel(tc, regional_means, adj, out):
     nc = tc.nc
     with ExitStack() as ctx:
         const = ctx.enter_context(tc.tile_pool(name="const", bufs=1))
-        a_pool = ctx.enter_context(tc.tile_pool(name="a_in", bufs=3))
-        r_pool = ctx.enter_context(tc.tile_pool(name="r_in", bufs=R_BUFS))
-        ga_pool = ctx.enter_context(tc.tile_pool(name="ga", bufs=2))
-        gr_pool = ctx.enter_context(tc.tile_pool(name="gr", bufs=3))
+        a_pool = ctx.enter_context(tc.tile_pool(name="a_in", bufs=LEAD))
+        r_pool = ctx.enter_context(tc.tile_pool(name="r_in", bufs=LEAD))
+        g_pool = ctx.enter_context(tc.tile_pool(name="grouped", bufs=3))
         q_pool = ctx.enter_context(tc.tile_pool(name="quant", bufs=3))
         o_pool = ctx.enter_context(tc.tile_pool(name="o_out", bufs=OUT_BUFS))
         ps_t = ctx.enter_context(tc.psum_pool(name="ps_t", bufs=4))
         ps_o = ctx.enter_context(tc.psum_pool(name="ps_o", bufs=4))
-        ctx.enter_context(tc.manual_schedule())
 
         a_in = {}
         r_in = {}
+        banks_t = {}
         g_a = {}
         g_r = {}
+        q_a = {}
+        q_r = {}
 
-        def load_group(g):
-            ag = a_pool.tile([P, ROWS * (N + 1)], BF16, name="ag")
-            nc.sync.dma_start(
-                out=ag[:, 0 : ROWS * N],
-                in_=adj[G * g : G * g + G].rearrange("b (s r) j -> (b s) (r j)", s=S),
-            )
-            a_in[g] = ag
-
-        def load_r(b):
+        def load(b):
+            a = a_pool.tile([P, PACK * N], BF16, name="a")
+            nc.sync.dma_start(out=a[:], in_=adj[b].rearrange("(p t) j -> p (t j)", t=PACK))
+            a_in[b] = a
             r = r_pool.tile([P, PACK * F], BF16, name="r")
             nc.sync.dma_start(
                 out=r[:], in_=regional_means[b].rearrange("(p t) f -> p (t f)", t=PACK)
             )
             r_in[b] = r
 
-        load_group(0)
-        load_r(0)
-        load_group(1)
-        for b in range(1, 6):
-            load_r(b)
-        load_group(2)
-        for b in range(6, R_BUFS):
-            load_r(b)
-        late_loads = [(load_group, 3), (load_r, 12), (load_r, 13), (load_r, 14), (load_r, 15)]
+        for b in range(LEAD):
+            load(b)
 
         ident = const.tile([P, P], F32, name="ident")
         make_identity(nc, ident[:])
-        hit = const.tile([P, S], F32, name="hit")
-        nc.vector.tensor_reduce(
-            out=hit[:],
-            in_=ident[:].rearrange("p (b c) -> p c b", c=S),
-            axis=mybir.AxisListType.X,
-            op=ADD,
-        )
-        keep = const.tile([P, S], BF16, name="keep")
-        nc.vector.tensor_scalar(
-            out=keep[:], in0=hit[:], scalar1=-1.0, scalar2=1.0, op0=MULT, op1=ADD
-        )
-        keep_rows = keep[:].unsqueeze(1).to_broadcast([P, PACK, S])
+        mask = const.tile([P, PACK, P, PACK], BF16, name="mask")
+        nc.vector.memset(mask[:], 1.0)
+        for t in range(PACK):
+            nc.vector.tensor_scalar(
+                out=mask[:, t, :, t], in0=ident[:], scalar1=-1.0, scalar2=1.0, op0=MULT, op1=ADD
+            )
+        mask_flat = mask[:].rearrange("p t c s -> p (t c s)")
 
-        def part(g, t):
-            ag = a_in[g]
-            if t == 0:
-                g_a[g] = ga_pool.tile([P, G * PACK * P * PACK], BF16, name="ga", align_bytes=64)
-            ga_words = g_a[g][:].bitcast(F32).rearrange(
-                "q (b t s m u) -> q b t s m u", b=G, t=PACK, s=S, u=2
-            )
-            diag = (
-                ag[:]
-                .rearrange("p (r x) -> p r x", x=N + 1)[:, :, 0:N]
-                .rearrange("p r (c y) -> p r c y", c=S)[:, :, :, 0]
-                .rearrange("p (m t) c -> p m t c", t=PACK)[:, :, t, :]
-            )
-            nc.vector.tensor_tensor(out=diag, in0=diag, in1=keep_rows, op=MULT)
-            words = ag[:, 0 : ROWS * N].bitcast(F32).rearrange("p (r c u) -> p r c u", r=ROWS, u=2)
-            for mh in range(2):
+        def mask_mul(b):
+            a = a_in[b]
+            nc.vector.tensor_tensor(out=a[:], in0=a[:], in1=mask_flat, op=MULT)
+
+        def transposes(b):
+            words = a_in[b][:].bitcast(F32).rearrange("p (t c u) -> p t c u", t=PACK, u=2)
+            banks = []
+            for h in range(2):
                 bank = ps_t.tile([P, 2, 2, P], F32, name="bank_t")
-                for m2 in range(2):
+                for t2 in range(2):
                     for u in range(2):
-                        nc.tensor.transpose(
-                            bank[:, m2, u, :], words[:, PACK * (2 * mh + m2) + t, :, u], ident[:]
-                        )
-                dst = ga_words[:, :, t, :, 2 * mh : 2 * mh + 2, :]
-                src = bank[:].rearrange("q m u (b s) -> q b s m u", s=S)
-                if t == PACK - 1:
-                    nc.vector.tensor_copy(out=dst, in_=src)
-                else:
-                    nc.scalar.copy(out=dst, in_=src)
+                        nc.tensor.transpose(bank[:, t2, u, :], words[:, 2 * h + t2, :, u], ident[:])
+                banks.append(bank)
+            banks_t[b] = banks
+
+        def copy_t(b):
+            ga = g_pool.tile([P, PACK * P * PACK], BF16, name="ga", align_bytes=64)
+            ga_words = ga[:].bitcast(F32).rearrange("q (t m u) -> q t m u", t=PACK, u=2)
+            for h in range(2):
+                nc.scalar.copy(
+                    out=ga_words[:, 2 * h : 2 * h + 2, :, :],
+                    in_=banks_t[b][h][:].rearrange("q t u m -> q t m u"),
+                )
+            g_a[b] = ga
 
         def regroup(b):
-            gr = gr_pool.tile([P, F * PACK], BF16, name="gr", align_bytes=64)
+            gr = g_pool.tile([P, F * PACK], BF16, name="gr", align_bytes=64)
             nc.vector.tensor_copy(
                 out=gr[:].rearrange("p (c i t) -> p c t i", i=4, t=PACK),
                 in_=r_in[b][:].rearrange("p (t c i) -> p c t i", t=PACK, i=4),
@@ -123,10 +99,12 @@ def tile_gcn_t_kernel(tc, regional_means, adj, out):
         def quantise(grouped, width, label):
             codes = q_pool.tile([P, width], U32, name="codes_" + label, align_bytes=64)
             scales = q_pool.tile([P, width], U8, name="scales_" + label, align_bytes=64)
-            nc.vector.quantize_mx(out=codes[:].bitcast(FP8X4), scales=scales[:], in_=grouped)
+            nc.vector.quantize_mx(out=codes[:].bitcast(FP8X4), scales=scales[:], in_=grouped[:])
             return codes, scales
 
-        def multiply_and_store(b, ca, sa, cr, sr):
+        def multiply_and_store(b):
+            ca, sa = q_a[b]
+            cr, sr = q_r[b]
             o = o_pool.tile([P, PACK * F], F32, name="o")
             accs = []
             for t in range(PACK):
@@ -146,19 +124,19 @@ def tile_gcn_t_kernel(tc, regional_means, adj, out):
                 nc.scalar.copy(out=o[:, t * F : (t + 1) * F], in_=accs[t][:])
             nc.sync.dma_start(out=out[b].rearrange("(p t) f -> p (t f)", t=PACK), in_=o[:])
 
-        for t in range(PACK):
-            part(0, t)
+        mask_mul(0)
+        transposes(0)
+        copy_t(0)
         regroup(0)
-        width = PACK * P * PACK
         for b in range(B):
-            g, k = divmod(b, G)
-            if g + 1 < GROUPS:
-                part(g + 1, k)
-            ca, sa = quantise(g_a[g][:, k * width : (k + 1) * width], N, "a")
-            cr, sr = quantise(g_r[b][:], F, "r")
             if b + 1 < B:
+                mask_mul(b + 1)
+                transposes(b + 1)
+            q_a[b] = quantise(g_a[b], N, "a")
+            q_r[b] = quantise(g_r[b], F, "r")
+            if b + 1 < B:
+                copy_t(b + 1)
                 regroup(b + 1)
-            multiply_and_store(b, ca, sa, cr, sr)
-            if b < len(late_loads):
-                fn, arg = late_loads[b]
-                fn(arg)
+            multiply_and_store(b)
+            if b + LEAD < B:
+                load(b + LEAD)

from contextlib import ExitStack

import concourse.mybir as mybir
from concourse.masks import make_identity

BF16 = mybir.dt.bfloat16
F32 = mybir.dt.float32
U32 = mybir.dt.uint32
U8 = mybir.dt.uint8
FP8X4 = mybir.dt.float8_e4m3fn_x4
MULT = mybir.AluOpType.mult
ADD = mybir.AluOpType.add

P = 128
PACK = 4
B, N, F = 16, 512, 512
FLOPS = 2 * B * N * N * F

LEAD = 12
OUT_BUFS = 8


def tile_gcn_t_kernel(tc, regional_means, adj, out):
    nc = tc.nc
    with ExitStack() as ctx:
        const = ctx.enter_context(tc.tile_pool(name="const", bufs=1))
        a_pool = ctx.enter_context(tc.tile_pool(name="a_in", bufs=LEAD))
        r_pool = ctx.enter_context(tc.tile_pool(name="r_in", bufs=LEAD))
        g_pool = ctx.enter_context(tc.tile_pool(name="grouped", bufs=3))
        q_pool = ctx.enter_context(tc.tile_pool(name="quant", bufs=3))
        o_pool = ctx.enter_context(tc.tile_pool(name="o_out", bufs=OUT_BUFS))
        ps_t = ctx.enter_context(tc.psum_pool(name="ps_t", bufs=4))
        ps_o = ctx.enter_context(tc.psum_pool(name="ps_o", bufs=4))

        a_in = {}
        r_in = {}
        banks_t = {}
        g_a = {}
        g_r = {}
        q_a = {}
        q_r = {}

        def load(b):
            a = a_pool.tile([P, PACK * N], BF16, name="a")
            nc.sync.dma_start(out=a[:], in_=adj[b].rearrange("(p t) j -> p (t j)", t=PACK))
            a_in[b] = a
            r = r_pool.tile([P, PACK * F], BF16, name="r")
            nc.sync.dma_start(
                out=r[:], in_=regional_means[b].rearrange("(p t) f -> p (t f)", t=PACK)
            )
            r_in[b] = r

        for b in range(LEAD):
            load(b)

        ident = const.tile([P, P], F32, name="ident")
        make_identity(nc, ident[:])
        mask = const.tile([P, PACK, P, PACK], BF16, name="mask")
        nc.vector.memset(mask[:], 1.0)
        for t in range(PACK):
            nc.vector.tensor_scalar(
                out=mask[:, t, :, t], in0=ident[:], scalar1=-1.0, scalar2=1.0, op0=MULT, op1=ADD
            )
        mask_flat = mask[:].rearrange("p t c s -> p (t c s)")

        def mask_mul(b):
            a = a_in[b]
            nc.vector.tensor_tensor(out=a[:], in0=a[:], in1=mask_flat, op=MULT)

        def transposes(b):
            words = a_in[b][:].bitcast(F32).rearrange("p (t c u) -> p t c u", t=PACK, u=2)
            banks = []
            for h in range(2):
                bank = ps_t.tile([P, 2, 2, P], F32, name="bank_t")
                for t2 in range(2):
                    for u in range(2):
                        nc.tensor.transpose(bank[:, t2, u, :], words[:, 2 * h + t2, :, u], ident[:])
                banks.append(bank)
            banks_t[b] = banks

        def copy_t(b):
            ga = g_pool.tile([P, PACK * P * PACK], BF16, name="ga", align_bytes=64)
            ga_words = ga[:].bitcast(F32).rearrange("q (t m u) -> q t m u", t=PACK, u=2)
            for h in range(2):
                nc.scalar.copy(
                    out=ga_words[:, 2 * h : 2 * h + 2, :, :],
                    in_=banks_t[b][h][:].rearrange("q t u m -> q t m u"),
                )
            g_a[b] = ga

        def regroup(b):
            gr = g_pool.tile([P, F * PACK], BF16, name="gr", align_bytes=64)
            nc.vector.tensor_copy(
                out=gr[:].rearrange("p (c i t) -> p c t i", i=4, t=PACK),
                in_=r_in[b][:].rearrange("p (t c i) -> p c t i", t=PACK, i=4),
            )
            g_r[b] = gr

        def quantise(grouped, width, label):
            codes = q_pool.tile([P, width], U32, name="codes_" + label, align_bytes=64)
            scales = q_pool.tile([P, width], U8, name="scales_" + label, align_bytes=64)
            nc.vector.quantize_mx(out=codes[:].bitcast(FP8X4), scales=scales[:], in_=grouped[:])
            return codes, scales

        def multiply_and_store(b):
            ca, sa = q_a[b]
            cr, sr = q_r[b]
            o = o_pool.tile([P, PACK * F], F32, name="o")
            accs = []
            for t in range(PACK):
                acc = ps_o.tile([P, F], F32, name="acc")
                cols = slice(t * P, (t + 1) * P)
                nc.tensor.matmul_mx(
                    out=acc[:],
                    lhsT=ca[:, cols].bitcast(FP8X4),
                    lhsT_scale=sa[:, cols],
                    rhs=cr[:].bitcast(FP8X4),
                    rhs_scale=sr[:],
                    start=True,
                    stop=True,
                )
                accs.append(acc)
            for t in range(PACK):
                nc.scalar.copy(out=o[:, t * F : (t + 1) * F], in_=accs[t][:])
            nc.sync.dma_start(out=out[b].rearrange("(p t) f -> p (t f)", t=PACK), in_=o[:])

        mask_mul(0)
        transposes(0)
        copy_t(0)
        regroup(0)
        for b in range(B):
            if b + 1 < B:
                mask_mul(b + 1)
                transposes(b + 1)
            q_a[b] = quantise(g_a[b], N, "a")
            q_r[b] = quantise(g_r[b], F, "r")
            if b + 1 < B:
                copy_t(b + 1)
                regroup(b + 1)
            multiply_and_store(b)
            if b + LEAD < B:
                load(b + LEAD)
